import numpy as np
import ml_dtypes

BF16 = ml_dtypes.bfloat16


def bf(x):
    return np.asarray(x, np.float32).astype(BF16)


def f32(x):
    return np.asarray(x, np.float32)


def f64(x):
    return np.asarray(x).astype(np.float64)


def striped(idx):
    return np.tile(idx.reshape(-1, 16).T, (8, 1))


S, D, HID, M, DOUT, N = 256, 128, 128, 256, 128, 128
LOG_SCALE_CLAMP = 2.0


def setup_inputs():
    return {
        "table": bf(np.random.standard_normal((S, D))),
        "w": bf(np.random.standard_normal((D, M)) / np.sqrt(D)),
        "b_in": f32(0.1 * np.random.standard_normal((M, 1))),
        "s_wout": bf(1.5 * np.random.standard_normal((HID, DOUT)) / np.sqrt(HID)),
        "s_bout": f32(0.1 * np.random.standard_normal((DOUT, 1))),
        "t_wout": bf(1.5 * np.random.standard_normal((HID, DOUT)) / np.sqrt(HID)),
        "t_bout": f32(0.1 * np.random.standard_normal((DOUT, 1))),
        "z2": f32(np.random.standard_normal((DOUT, N))),
        "offs": striped(np.random.permutation(S)[:N]),
    }


def reference(table, w, b_in, s_wout, s_bout, t_wout, t_bout, z2, offs):
    idx = offs[:16].T.reshape(-1)
    h = np.maximum(f64(w).T @ f64(table)[idx].T + f64(b_in), 0.0)
    log_s = np.minimum(np.maximum(f64(s_wout).T @ h[:HID] + f64(s_bout), -LOG_SCALE_CLAMP), LOG_SCALE_CLAMP)
    t = f64(t_wout).T @ h[HID:] + f64(t_bout)
    return f64(z2) * np.exp(log_s) + t

@@ -1,0 +1,81 @@
+import concourse.mybir as mybir
+from concourse.masks import make_identity
+
+P = 128
+S = 256
+D = 128
+HID = 128
+DOUT = 128
+N = 128
+CLAMP = 2.0
+
+BF16, F32, U16 = mybir.dt.bfloat16, mybir.dt.float32, mybir.dt.uint16
+ADD, MULT = mybir.AluOpType.add, mybir.AluOpType.mult
+MAX, MIN = mybir.AluOpType.max, mybir.AluOpType.min
+RELU, EXP = mybir.ActivationFunctionType.Relu, mybir.ActivationFunctionType.Exp
+
+FLOPS = 2 * D * (2 * HID) * N + 2 * (2 * HID * DOUT * N)
+
+
+def tile_affinecouplinglayer_kernel(
+    tc, table, w, b_in, s_wout, s_bout, t_wout, t_bout, z2, offs, out
+):
+    nc = tc.nc
+    with (
+        tc.tile_pool(name="held", bufs=1) as held,
+        tc.psum_pool(name="psum", bufs=1) as psum,
+    ):
+        samples = held.tile([P, S // P, D], BF16, name="samples")
+        nc.sync.dma_start(samples[:], table.rearrange("(b p) d -> p b d", p=P))
+        offsets = held.tile([P, N // 16], U16, name="offsets")
+        nc.sync.dma_start(offsets[:], offs)
+        w_in = held.tile([D, 2 * HID], BF16, name="w_in")
+        nc.scalar.dma_start(w_in[:], w)
+        bias_hs = held.tile([HID, 1], F32, name="bias_hs")
+        nc.scalar.dma_start(bias_hs[:], b_in[0:HID, :])
+        bias_ht = held.tile([HID, 1], F32, name="bias_ht")
+        nc.scalar.dma_start(bias_ht[:], b_in[HID : 2 * HID, :])
+        w_s = held.tile([HID, DOUT], BF16, name="w_s")
+        nc.sync.dma_start(w_s[:], s_wout)
+        w_t = held.tile([HID, DOUT], BF16, name="w_t")
+        nc.sync.dma_start(w_t[:], t_wout)
+        bias_s = held.tile([DOUT, 1], F32, name="bias_s")
+        nc.scalar.dma_start(bias_s[:], s_bout)
+        bias_t = held.tile([DOUT, 1], F32, name="bias_t")
+        nc.scalar.dma_start(bias_t[:], t_bout)
+        other_half = held.tile([DOUT, N], F32, name="other_half")
+        nc.sync.dma_start(other_half[:], z2)
+
+        identity = held.tile([P, P], BF16, name="identity")
+        make_identity(nc, identity[:])
+        flipped = psum.tile([D, S], BF16, name="flipped")
+        for b in range(S // P):
+            nc.tensor.transpose(flipped[:, b * P : (b + 1) * P], samples[:, b, :], identity[:])
+        window = held.tile([D, S], BF16, name="window")
+        nc.vector.tensor_copy(window[:], flipped[:])
+
+        hs_sum = psum.tile([HID, N], F32, name="hs_sum")
+        nc.tensor.matmul(hs_sum[:], w_in[:, 0:HID], window[:].indirect(offsets[:]))
+        ht_sum = psum.tile([HID, N], F32, name="ht_sum")
+        nc.tensor.matmul(ht_sum[:], w_in[:, HID : 2 * HID], window[:].indirect(offsets[:]))
+
+        h_s = held.tile([HID, N], BF16, name="h_s")
+        nc.vector.tensor_scalar(h_s[:], hs_sum[:], bias_hs[:], 0.0, ADD, MAX)
+        h_t = held.tile([HID, N], BF16, name="h_t")
+        nc.scalar.activation(h_t[:], ht_sum[:], RELU, bias=bias_ht[:])
+
+        s_sum = psum.tile([DOUT, N], F32, name="s_sum")
+        nc.tensor.matmul(s_sum[:], w_s[:], h_s[:])
+        t_sum = psum.tile([DOUT, N], F32, name="t_sum")
+        nc.tensor.matmul(t_sum[:], w_t[:], h_t[:])
+
+        log_s = held.tile([DOUT, N], F32, name="log_s")
+        nc.vector.tensor_scalar(log_s[:], s_sum[:], bias_s[:], -CLAMP, ADD, MAX)
+        nc.vector.tensor_scalar_min(log_s[:], log_s[:], CLAMP)
+        scale = held.tile([DOUT, N], F32, name="scale")
+        nc.scalar.activation(scale[:], log_s[:], EXP)
+        scaled = held.tile([DOUT, N], F32, name="scaled")
+        nc.vector.tensor_tensor(scaled[:], other_half[:], scale[:], MULT)
+        result = held.tile([DOUT, N], F32, name="result")
+        nc.vector.scalar_tensor_tensor(result[:], t_sum[:], bias_t[:], scaled[:], ADD, ADD)
+        nc.sync.dma_start(out, result[:])

@@ -32,22 +32,27 @@ def tile_affinecouplinglayer_kernel(
         w_in = held.tile([D, 2 * HID], BF16, name="w_in")
         nc.scalar.dma_start(w_in[:], w)
         bias_hs = held.tile([HID, 1], F32, name="bias_hs")
-        nc.scalar.dma_start(bias_hs[:], b_in[0:HID, :])
+        nc.sync.dma_start(bias_hs[:], b_in[0:HID, :])
         bias_ht = held.tile([HID, 1], F32, name="bias_ht")
-        nc.scalar.dma_start(bias_ht[:], b_in[HID : 2 * HID, :])
+        nc.sync.dma_start(bias_ht[:], b_in[HID : 2 * HID, :])
         w_s = held.tile([HID, DOUT], BF16, name="w_s")
         nc.sync.dma_start(w_s[:], s_wout)
         w_t = held.tile([HID, DOUT], BF16, name="w_t")
-        nc.sync.dma_start(w_t[:], t_wout)
-        bias_s = held.tile([DOUT, 1], F32, name="bias_s")
-        nc.scalar.dma_start(bias_s[:], s_bout)
-        bias_t = held.tile([DOUT, 1], F32, name="bias_t")
-        nc.scalar.dma_start(bias_t[:], t_bout)
-        other_half = held.tile([DOUT, N], F32, name="other_half")
-        nc.sync.dma_start(other_half[:], z2)
+        nc.scalar.dma_start(w_t[:], t_wout)
 
         identity = held.tile([P, P], BF16, name="identity")
         make_identity(nc, identity[:])
+        bias_s = held.tile([DOUT, 1], F32, name="bias_s")
+        nc.gpsimd.dma_start(bias_s[:], s_bout)
+        other_half = held.tile([DOUT, N], F32, name="other_half")
+        nc.gpsimd.dma_start(other_half[:], z2)
+        bias_t = held.tile([DOUT, 1], F32, name="bias_t")
+        nc.gpsimd.dma_start(bias_t[:], t_bout)
+
+        floor = held.tile([DOUT, 1], F32, name="floor")
+        nc.vector.memset(floor[:], -CLAMP)
+        nc.scalar.activation(floor[:], floor[:], EXP)
+
         flipped = psum.tile([D, S], BF16, name="flipped")
         for b in range(S // P):
             nc.tensor.transpose(flipped[:, b * P : (b + 1) * P], samples[:, b, :], identity[:])
@@ -70,12 +75,11 @@ def tile_affinecouplinglayer_kernel(
         nc.tensor.matmul(t_sum[:], w_t[:], h_t[:])
 
         log_s = held.tile([DOUT, N], F32, name="log_s")
-        nc.vector.tensor_scalar(log_s[:], s_sum[:], bias_s[:], -CLAMP, ADD, MAX)
-        nc.vector.tensor_scalar_min(log_s[:], log_s[:], CLAMP)
+        nc.vector.tensor_scalar(log_s[:], s_sum[:], bias_s[:], CLAMP, ADD, MIN)
         scale = held.tile([DOUT, N], F32, name="scale")
         nc.scalar.activation(scale[:], log_s[:], EXP)
         scaled = held.tile([DOUT, N], F32, name="scaled")
-        nc.vector.tensor_tensor(scaled[:], other_half[:], scale[:], MULT)
+        nc.vector.scalar_tensor_tensor(scaled[:], scale[:], floor[:], other_half[:], MAX, MULT)
         result = held.tile([DOUT, N], F32, name="result")
         nc.vector.scalar_tensor_tensor(result[:], t_sum[:], bias_t[:], scaled[:], ADD, ADD)
         nc.sync.dma_start(out, result[:])

@@ -8,6 +8,8 @@ HID = 128
 DOUT = 128
 N = 128
 CLAMP = 2.0
+BANK = 512
+WARM_UP = 4
 
 BF16, F32, U16 = mybir.dt.bfloat16, mybir.dt.float32, mybir.dt.uint16
 ADD, MULT = mybir.AluOpType.add, mybir.AluOpType.mult
@@ -31,23 +33,28 @@ def tile_affinecouplinglayer_kernel(
         nc.sync.dma_start(offsets[:], offs)
         w_in = held.tile([D, 2 * HID], BF16, name="w_in")
         nc.scalar.dma_start(w_in[:], w)
-        bias_hs = held.tile([HID, 1], F32, name="bias_hs")
-        nc.sync.dma_start(bias_hs[:], b_in[0:HID, :])
-        bias_ht = held.tile([HID, 1], F32, name="bias_ht")
-        nc.sync.dma_start(bias_ht[:], b_in[HID : 2 * HID, :])
         w_s = held.tile([HID, DOUT], BF16, name="w_s")
-        nc.sync.dma_start(w_s[:], s_wout)
+        nc.scalar.dma_start(w_s[:], s_wout)
         w_t = held.tile([HID, DOUT], BF16, name="w_t")
         nc.scalar.dma_start(w_t[:], t_wout)
+        bias_h = held.tile([HID, 2], F32, name="bias_h")
+        with nc.allow_non_contiguous_dma(reason="one float32 to a partition from each half of b_in"):
+            nc.sync.dma_start(bias_h[:], b_in.rearrange("(net k) one -> k (net one)", k=HID))
+        bias_s = held.tile([DOUT, 1], F32, name="bias_s")
+        nc.sync.dma_start(bias_s[:], s_bout)
+        other_half = held.tile([DOUT, N], F32, name="other_half")
+        nc.sync.dma_start(other_half[:], z2)
+        bias_t = held.tile([DOUT, 1], F32, name="bias_t")
+        nc.sync.dma_start(bias_t[:], t_bout)
+
+        zeros = held.tile([P, BANK], BF16, name="zeros")
+        nc.gpsimd.memset(zeros[:], 0.0)
+        unused = psum.tile([P, BANK], F32, name="unused")
+        for turn in range(WARM_UP):
+            nc.tensor.matmul(unused[:], zeros[:, 0:P], zeros[:])
 
         identity = held.tile([P, P], BF16, name="identity")
         make_identity(nc, identity[:])
-        bias_s = held.tile([DOUT, 1], F32, name="bias_s")
-        nc.gpsimd.dma_start(bias_s[:], s_bout)
-        other_half = held.tile([DOUT, N], F32, name="other_half")
-        nc.gpsimd.dma_start(other_half[:], z2)
-        bias_t = held.tile([DOUT, 1], F32, name="bias_t")
-        nc.gpsimd.dma_start(bias_t[:], t_bout)
 
         floor = held.tile([DOUT, 1], F32, name="floor")
         nc.vector.memset(floor[:], -CLAMP)
@@ -65,9 +72,9 @@ def tile_affinecouplinglayer_kernel(
         nc.tensor.matmul(ht_sum[:], w_in[:, HID : 2 * HID], window[:].indirect(offsets[:]))
 
         h_s = held.tile([HID, N], BF16, name="h_s")
-        nc.vector.tensor_scalar(h_s[:], hs_sum[:], bias_hs[:], 0.0, ADD, MAX)
+        nc.vector.tensor_scalar(h_s[:], hs_sum[:], bias_h[:, 0:1], 0.0, ADD, MAX)
         h_t = held.tile([HID, N], BF16, name="h_t")
-        nc.scalar.activation(h_t[:], ht_sum[:], RELU, bias=bias_ht[:])
+        nc.scalar.activation(h_t[:], ht_sum[:], RELU, bias=bias_h[:, 1:2])
 
         s_sum = psum.tile([DOUT, N], F32, name="s_sum")
         nc.tensor.matmul(s_sum[:], w_s[:], h_s[:])

@@ -8,8 +8,6 @@ HID = 128
 DOUT = 128
 N = 128
 CLAMP = 2.0
-BANK = 512
-WARM_UP = 4
 
 BF16, F32, U16 = mybir.dt.bfloat16, mybir.dt.float32, mybir.dt.uint16
 ADD, MULT = mybir.AluOpType.add, mybir.AluOpType.mult
@@ -46,12 +44,6 @@ def tile_affinecouplinglayer_kernel(
         nc.sync.dma_start(other_half[:], z2)
         bias_t = held.tile([DOUT, 1], F32, name="bias_t")
         nc.sync.dma_start(bias_t[:], t_bout)
-
-        zeros = held.tile([P, BANK], BF16, name="zeros")
-        nc.gpsimd.memset(zeros[:], 0.0)
-        unused = psum.tile([P, BANK], F32, name="unused")
-        for turn in range(WARM_UP):
-            nc.tensor.matmul(unused[:], zeros[:, 0:P], zeros[:])
 
         identity = held.tile([P, P], BF16, name="identity")
         make_identity(nc, identity[:])

@@ -3,6 +3,7 @@ from concourse.masks import make_identity
 
 P = 128
 S = 256
+BLOCKS = S // P
 D = 128
 HID = 128
 DOUT = 128
@@ -25,8 +26,9 @@ def tile_affinecouplinglayer_kernel(
         tc.tile_pool(name="held", bufs=1) as held,
         tc.psum_pool(name="psum", bufs=1) as psum,
     ):
-        samples = held.tile([P, S // P, D], BF16, name="samples")
-        nc.sync.dma_start(samples[:], table.rearrange("(b p) d -> p b d", p=P))
+        samples = [held.tile([P, D], BF16, name=f"samples{b}") for b in range(BLOCKS)]
+        nc.sync.dma_start(samples[0][:], table[0:P, :])
+        nc.scalar.dma_start(samples[1][:], table[P : 2 * P, :])
         offsets = held.tile([P, N // 16], U16, name="offsets")
         nc.sync.dma_start(offsets[:], offs)
         w_in = held.tile([D, 2 * HID], BF16, name="w_in")
@@ -48,15 +50,19 @@ def tile_affinecouplinglayer_kernel(
         identity = held.tile([P, P], BF16, name="identity")
         make_identity(nc, identity[:])
 
-        floor = held.tile([DOUT, 1], F32, name="floor")
-        nc.vector.memset(floor[:], -CLAMP)
-        nc.scalar.activation(floor[:], floor[:], EXP)
+        bounds = held.tile([DOUT, 2], F32, name="bounds")
+        nc.vector.memset(bounds[:, 0:1], -CLAMP)
+        nc.vector.memset(bounds[:, 1:2], CLAMP)
+        nc.scalar.activation(bounds[:], bounds[:], EXP)
 
-        flipped = psum.tile([D, S], BF16, name="flipped")
-        for b in range(S // P):
-            nc.tensor.transpose(flipped[:, b * P : (b + 1) * P], samples[:, b, :], identity[:])
         window = held.tile([D, S], BF16, name="window")
-        nc.vector.tensor_copy(window[:], flipped[:])
+        for b in range(BLOCKS):
+            flipped = psum.tile([D, P], BF16, name=f"flipped{b}")
+            nc.tensor.transpose(flipped[:], samples[b][:], identity[:])
+            if b % 2 == 0:
+                nc.vector.tensor_copy(window[:, b * P : (b + 1) * P], flipped[:])
+            else:
+                nc.scalar.copy(window[:, b * P : (b + 1) * P], flipped[:])
 
         hs_sum = psum.tile([HID, N], F32, name="hs_sum")
         nc.tensor.matmul(hs_sum[:], w_in[:, 0:HID], window[:].indirect(offsets[:]))
@@ -73,12 +79,11 @@ def tile_affinecouplinglayer_kernel(
         t_sum = psum.tile([DOUT, N], F32, name="t_sum")
         nc.tensor.matmul(t_sum[:], w_t[:], h_t[:])
 
-        log_s = held.tile([DOUT, N], F32, name="log_s")
-        nc.vector.tensor_scalar(log_s[:], s_sum[:], bias_s[:], CLAMP, ADD, MIN)
         scale = held.tile([DOUT, N], F32, name="scale")
-        nc.scalar.activation(scale[:], log_s[:], EXP)
+        nc.scalar.activation(scale[:], s_sum[:], EXP, bias=bias_s[:])
+        nc.vector.tensor_scalar(scale[:], scale[:], bounds[:, 0:1], bounds[:, 1:2], MAX, MIN)
         scaled = held.tile([DOUT, N], F32, name="scaled")
-        nc.vector.scalar_tensor_tensor(scaled[:], scale[:], floor[:], other_half[:], MAX, MULT)
+        nc.vector.tensor_tensor(scaled[:], scale[:], other_half[:], MULT)
         result = held.tile([DOUT, N], F32, name="result")
         nc.vector.scalar_tensor_tensor(result[:], t_sum[:], bias_t[:], scaled[:], ADD, ADD)
         nc.sync.dma_start(out, result[:])

@@ -59,10 +59,7 @@ def tile_affinecouplinglayer_kernel(
         for b in range(BLOCKS):
             flipped = psum.tile([D, P], BF16, name=f"flipped{b}")
             nc.tensor.transpose(flipped[:], samples[b][:], identity[:])
-            if b % 2 == 0:
-                nc.vector.tensor_copy(window[:, b * P : (b + 1) * P], flipped[:])
-            else:
-                nc.scalar.copy(window[:, b * P : (b + 1) * P], flipped[:])
+            nc.vector.tensor_copy(window[:, b * P : (b + 1) * P], flipped[:])
 
         hs_sum = psum.tile([HID, N], F32, name="hs_sum")
         nc.tensor.matmul(hs_sum[:], w_in[:, 0:HID], window[:].indirect(offsets[:]))

@@ -9,6 +9,8 @@ HID = 128
 DOUT = 128
 N = 128
 CLAMP = 2.0
+HALF = N // 2
+HALVES = (slice(0, HALF), slice(HALF, N))
 
 BF16, F32, U16 = mybir.dt.bfloat16, mybir.dt.float32, mybir.dt.uint16
 ADD, MULT = mybir.AluOpType.add, mybir.AluOpType.mult
@@ -66,21 +68,29 @@ def tile_affinecouplinglayer_kernel(
         ht_sum = psum.tile([HID, N], F32, name="ht_sum")
         nc.tensor.matmul(ht_sum[:], w_in[:, HID : 2 * HID], window[:].indirect(offsets[:]))
 
+
         h_s = held.tile([HID, N], BF16, name="h_s")
-        nc.vector.tensor_scalar(h_s[:], hs_sum[:], bias_h[:, 0:1], 0.0, ADD, MAX)
+        for cols in HALVES:
+            nc.vector.tensor_scalar(h_s[:, cols], hs_sum[:, cols], bias_h[:, 0:1], 0.0, ADD, MAX)
         h_t = held.tile([HID, N], BF16, name="h_t")
         nc.scalar.activation(h_t[:], ht_sum[:], RELU, bias=bias_h[:, 1:2])
 
-        s_sum = psum.tile([DOUT, N], F32, name="s_sum")
-        nc.tensor.matmul(s_sum[:], w_s[:], h_s[:])
+        s_sums = [psum.tile([DOUT, HALF], F32, name=f"s_sum{i}") for i in range(len(HALVES))]
+        for s_sum, cols in zip(s_sums, HALVES):
+            nc.tensor.matmul(s_sum[:], w_s[:], h_s[:, cols])
         t_sum = psum.tile([DOUT, N], F32, name="t_sum")
         nc.tensor.matmul(t_sum[:], w_t[:], h_t[:])
 
         scale = held.tile([DOUT, N], F32, name="scale")
-        nc.scalar.activation(scale[:], s_sum[:], EXP, bias=bias_s[:])
-        nc.vector.tensor_scalar(scale[:], scale[:], bounds[:, 0:1], bounds[:, 1:2], MAX, MIN)
+        for s_sum, cols in zip(s_sums, HALVES):
+            nc.scalar.activation(scale[:, cols], s_sum[:], EXP, bias=bias_s[:])
+        clamped = held.tile([DOUT, N], F32, name="clamped")
+        for cols in HALVES:
+            nc.vector.tensor_scalar(clamped[:, cols], scale[:, cols], bounds[:, 0:1], bounds[:, 1:2], MAX, MIN)
         scaled = held.tile([DOUT, N], F32, name="scaled")
-        nc.vector.tensor_tensor(scaled[:], scale[:], other_half[:], MULT)
+        for cols in HALVES:
+            nc.vector.tensor_tensor(scaled[:, cols], clamped[:, cols], other_half[:, cols], MULT)
         result = held.tile([DOUT, N], F32, name="result")
-        nc.vector.scalar_tensor_tensor(result[:], t_sum[:], bias_t[:], scaled[:], ADD, ADD)
+        for cols in HALVES:
+            nc.vector.scalar_tensor_tensor(result[:, cols], t_sum[:, cols], bias_t[:], scaled[:, cols], ADD, ADD)
         nc.sync.dma_start(out, result[:])

@@ -63,15 +63,17 @@ def tile_affinecouplinglayer_kernel(
             nc.tensor.transpose(flipped[:], samples[b][:], identity[:])
             nc.vector.tensor_copy(window[:, b * P : (b + 1) * P], flipped[:])
 
-        hs_sum = psum.tile([HID, N], F32, name="hs_sum")
-        nc.tensor.matmul(hs_sum[:], w_in[:, 0:HID], window[:].indirect(offsets[:]))
+        hs_sums = [psum.tile([HID, HALF], F32, name=f"hs_sum{i}") for i in range(len(HALVES))]
+        for i, hs_sum in enumerate(hs_sums):
+            piece = offsets[:, i * (HALF // 16) : (i + 1) * (HALF // 16)]
+            nc.tensor.matmul(hs_sum[:], w_in[:, 0:HID], window[:].indirect(piece))
         ht_sum = psum.tile([HID, N], F32, name="ht_sum")
         nc.tensor.matmul(ht_sum[:], w_in[:, HID : 2 * HID], window[:].indirect(offsets[:]))
 
 
         h_s = held.tile([HID, N], BF16, name="h_s")
-        for cols in HALVES:
-            nc.vector.tensor_scalar(h_s[:, cols], hs_sum[:, cols], bias_h[:, 0:1], 0.0, ADD, MAX)
+        for hs_sum, cols in zip(hs_sums, HALVES):
+            nc.vector.tensor_scalar(h_s[:, cols], hs_sum[:], bias_h[:, 0:1], 0.0, ADD, MAX)
         h_t = held.tile([HID, N], BF16, name="h_t")
         nc.scalar.activation(h_t[:], ht_sum[:], RELU, bias=bias_h[:, 1:2])
 

@@ -1,3 +1,5 @@
+import math
+
 import concourse.mybir as mybir
 from concourse.masks import make_identity
 
@@ -52,10 +54,9 @@ def tile_affinecouplinglayer_kernel(
         identity = held.tile([P, P], BF16, name="identity")
         make_identity(nc, identity[:])
 
-        bounds = held.tile([DOUT, 2], F32, name="bounds")
-        nc.vector.memset(bounds[:, 0:1], -CLAMP)
-        nc.vector.memset(bounds[:, 1:2], CLAMP)
-        nc.scalar.activation(bounds[:], bounds[:], EXP)
+        warm = held.tile([P, 1], F32, name="warm")
+        nc.vector.memset(warm[:], 0.0)
+        nc.scalar.activation(warm[:], warm[:], EXP)
 
         window = held.tile([D, S], BF16, name="window")
         for b in range(BLOCKS):
@@ -88,7 +89,7 @@ def tile_affinecouplinglayer_kernel(
             nc.scalar.activation(scale[:, cols], s_sum[:], EXP, bias=bias_s[:])
         clamped = held.tile([DOUT, N], F32, name="clamped")
         for cols in HALVES:
-            nc.vector.tensor_scalar(clamped[:, cols], scale[:, cols], bounds[:, 0:1], bounds[:, 1:2], MAX, MIN)
+            nc.vector.tensor_scalar(clamped[:, cols], scale[:, cols], math.exp(-CLAMP), math.exp(CLAMP), MAX, MIN)
         scaled = held.tile([DOUT, N], F32, name="scaled")
         for cols in HALVES:
             nc.vector.tensor_tensor(scaled[:, cols], clamped[:, cols], other_half[:, cols], MULT)

@@ -13,6 +13,8 @@ N = 128
 CLAMP = 2.0
 HALF = N // 2
 HALVES = (slice(0, HALF), slice(HALF, N))
+QUARTER = N // 4
+QUARTERS = tuple(slice(q * QUARTER, (q + 1) * QUARTER) for q in range(4))
 
 BF16, F32, U16 = mybir.dt.bfloat16, mybir.dt.float32, mybir.dt.uint16
 ADD, MULT = mybir.AluOpType.add, mybir.AluOpType.mult
@@ -60,7 +62,7 @@ def tile_affinecouplinglayer_kernel(
 
         window = held.tile([D, S], BF16, name="window")
         for b in range(BLOCKS):
-            flipped = psum.tile([D, P], BF16, name=f"flipped{b}")
+            flipped = psum.tile([D, P], BF16, name=f"flipped{b}", tag=f"bank{b}")
             nc.tensor.transpose(flipped[:], samples[b][:], identity[:])
             nc.vector.tensor_copy(window[:, b * P : (b + 1) * P], flipped[:])
 
@@ -73,27 +75,28 @@ def tile_affinecouplinglayer_kernel(
 
 
         h_s = held.tile([HID, N], BF16, name="h_s")
-        for hs_sum, cols in zip(hs_sums, HALVES):
-            nc.vector.tensor_scalar(h_s[:, cols], hs_sum[:], bias_h[:, 0:1], 0.0, ADD, MAX)
+        for q, cols in enumerate(QUARTERS):
+            in_half = slice((q % 2) * QUARTER, (q % 2 + 1) * QUARTER)
+            nc.vector.tensor_scalar(h_s[:, cols], hs_sums[q // 2][:, in_half], bias_h[:, 0:1], 0.0, ADD, MAX)
         h_t = held.tile([HID, N], BF16, name="h_t")
         nc.scalar.activation(h_t[:], ht_sum[:], RELU, bias=bias_h[:, 1:2])
 
-        s_sums = [psum.tile([DOUT, HALF], F32, name=f"s_sum{i}") for i in range(len(HALVES))]
-        for s_sum, cols in zip(s_sums, HALVES):
+        s_sums = [psum.tile([DOUT, QUARTER], F32, name=f"s_sum{q}", tag=f"bank{q}") for q in range(len(QUARTERS))]
+        for s_sum, cols in zip(s_sums, QUARTERS):
             nc.tensor.matmul(s_sum[:], w_s[:], h_s[:, cols])
         t_sum = psum.tile([DOUT, N], F32, name="t_sum")
         nc.tensor.matmul(t_sum[:], w_t[:], h_t[:])
 
         scale = held.tile([DOUT, N], F32, name="scale")
-        for s_sum, cols in zip(s_sums, HALVES):
+        for s_sum, cols in zip(s_sums, QUARTERS):
             nc.scalar.activation(scale[:, cols], s_sum[:], EXP, bias=bias_s[:])
         clamped = held.tile([DOUT, N], F32, name="clamped")
-        for cols in HALVES:
+        for cols in QUARTERS:
             nc.vector.tensor_scalar(clamped[:, cols], scale[:, cols], math.exp(-CLAMP), math.exp(CLAMP), MAX, MIN)
         scaled = held.tile([DOUT, N], F32, name="scaled")
-        for cols in HALVES:
+        for cols in QUARTERS:
             nc.vector.tensor_tensor(scaled[:, cols], clamped[:, cols], other_half[:, cols], MULT)
         result = held.tile([DOUT, N], F32, name="result")
-        for cols in HALVES:
+        for cols in QUARTERS:
             nc.vector.scalar_tensor_tensor(result[:, cols], t_sum[:, cols], bias_t[:], scaled[:, cols], ADD, ADD)
         nc.sync.dma_start(out, result[:])

@@ -97,6 +97,6 @@ def tile_affinecouplinglayer_kernel(
         for cols in QUARTERS:
             nc.vector.tensor_tensor(scaled[:, cols], clamped[:, cols], other_half[:, cols], MULT)
         result = held.tile([DOUT, N], F32, name="result")
-        for cols in QUARTERS:
+        for cols in HALVES:
             nc.vector.scalar_tensor_tensor(result[:, cols], t_sum[:, cols], bias_t[:], scaled[:, cols], ADD, ADD)
         nc.sync.dma_start(out, result[:])

@@ -34,18 +34,18 @@ def tile_affinecouplinglayer_kernel(
     ):
         samples = [held.tile([P, D], BF16, name=f"samples{b}") for b in range(BLOCKS)]
         nc.sync.dma_start(samples[0][:], table[0:P, :])
-        nc.scalar.dma_start(samples[1][:], table[P : 2 * P, :])
+        nc.sync.dma_start(samples[1][:], table[P : 2 * P, :])
         offsets = held.tile([P, N // 16], U16, name="offsets")
         nc.sync.dma_start(offsets[:], offs)
         w_in = held.tile([D, 2 * HID], BF16, name="w_in")
-        nc.scalar.dma_start(w_in[:], w)
-        w_s = held.tile([HID, DOUT], BF16, name="w_s")
-        nc.scalar.dma_start(w_s[:], s_wout)
-        w_t = held.tile([HID, DOUT], BF16, name="w_t")
-        nc.scalar.dma_start(w_t[:], t_wout)
+        nc.sync.dma_start(w_in[:], w)
         bias_h = held.tile([HID, 2], F32, name="bias_h")
         with nc.allow_non_contiguous_dma(reason="one float32 to a partition from each half of b_in"):
             nc.sync.dma_start(bias_h[:], b_in.rearrange("(net k) one -> k (net one)", k=HID))
+        w_s = held.tile([HID, DOUT], BF16, name="w_s")
+        nc.sync.dma_start(w_s[:], s_wout)
+        w_t = held.tile([HID, DOUT], BF16, name="w_t")
+        nc.sync.dma_start(w_t[:], t_wout)
         bias_s = held.tile([DOUT, 1], F32, name="bias_s")
         nc.sync.dma_start(bias_s[:], s_bout)
         other_half = held.tile([DOUT, N], F32, name="other_half")

@@ -96,7 +96,7 @@ def tile_affinecouplinglayer_kernel(
         scaled = held.tile([DOUT, N], F32, name="scaled")
         for cols in QUARTERS:
             nc.vector.tensor_tensor(scaled[:, cols], clamped[:, cols], other_half[:, cols], MULT)
-        result = held.tile([DOUT, N], F32, name="result")
-        for cols in HALVES:
-            nc.vector.scalar_tensor_tensor(result[:, cols], t_sum[:, cols], bias_t[:], scaled[:, cols], ADD, ADD)
-        nc.sync.dma_start(out, result[:])
+        for i, cols in enumerate(HALVES):
+            result = held.tile([DOUT, HALF], F32, name=f"result{i}")
+            nc.vector.scalar_tensor_tensor(result[:], t_sum[:, cols], bias_t[:], scaled[:, cols], ADD, ADD)
+            nc.sync.dma_start(out[:, cols], result[:])

@@ -96,7 +96,11 @@ def tile_affinecouplinglayer_kernel(
         scaled = held.tile([DOUT, N], F32, name="scaled")
         for cols in QUARTERS:
             nc.vector.tensor_tensor(scaled[:, cols], clamped[:, cols], other_half[:, cols], MULT)
-        for i, cols in enumerate(HALVES):
-            result = held.tile([DOUT, HALF], F32, name=f"result{i}")
-            nc.vector.scalar_tensor_tensor(result[:], t_sum[:, cols], bias_t[:], scaled[:, cols], ADD, ADD)
+        results = [held.tile([DOUT, HALF], F32, name=f"result{i}") for i in range(len(HALVES))]
+        for q, cols in enumerate(QUARTERS):
+            in_half = slice((q % 2) * QUARTER, (q % 2 + 1) * QUARTER)
+            nc.vector.scalar_tensor_tensor(
+                results[q // 2][:, in_half], t_sum[:, cols], bias_t[:], scaled[:, cols], ADD, ADD
+            )
+        for result, cols in zip(results, HALVES):
             nc.sync.dma_start(out[:, cols], result[:])

import math

import concourse.mybir as mybir
from concourse.masks import make_identity

P = 128
S = 256
BLOCKS = S // P
D = 128
HID = 128
DOUT = 128
N = 128
CLAMP = 2.0
HALF = N // 2
HALVES = (slice(0, HALF), slice(HALF, N))
QUARTER = N // 4
QUARTERS = tuple(slice(q * QUARTER, (q + 1) * QUARTER) for q in range(4))

BF16, F32, U16 = mybir.dt.bfloat16, mybir.dt.float32, mybir.dt.uint16
ADD, MULT = mybir.AluOpType.add, mybir.AluOpType.mult
MAX, MIN = mybir.AluOpType.max, mybir.AluOpType.min
RELU, EXP = mybir.ActivationFunctionType.Relu, mybir.ActivationFunctionType.Exp

FLOPS = 2 * D * (2 * HID) * N + 2 * (2 * HID * DOUT * N)


def tile_affinecouplinglayer_kernel(
    tc, table, w, b_in, s_wout, s_bout, t_wout, t_bout, z2, offs, out
):
    nc = tc.nc
    with (
        tc.tile_pool(name="held", bufs=1) as held,
        tc.psum_pool(name="psum", bufs=1) as psum,
    ):
        samples = [held.tile([P, D], BF16, name=f"samples{b}") for b in range(BLOCKS)]
        nc.sync.dma_start(samples[0][:], table[0:P, :])
        nc.sync.dma_start(samples[1][:], table[P : 2 * P, :])
        offsets = held.tile([P, N // 16], U16, name="offsets")
        nc.sync.dma_start(offsets[:], offs)
        w_in = held.tile([D, 2 * HID], BF16, name="w_in")
        nc.sync.dma_start(w_in[:], w)
        bias_h = held.tile([HID, 2], F32, name="bias_h")
        with nc.allow_non_contiguous_dma(reason="one float32 to a partition from each half of b_in"):
            nc.sync.dma_start(bias_h[:], b_in.rearrange("(net k) one -> k (net one)", k=HID))
        w_s = held.tile([HID, DOUT], BF16, name="w_s")
        nc.sync.dma_start(w_s[:], s_wout)
        w_t = held.tile([HID, DOUT], BF16, name="w_t")
        nc.sync.dma_start(w_t[:], t_wout)
        bias_s = held.tile([DOUT, 1], F32, name="bias_s")
        nc.sync.dma_start(bias_s[:], s_bout)
        other_half = held.tile([DOUT, N], F32, name="other_half")
        nc.sync.dma_start(other_half[:], z2)
        bias_t = held.tile([DOUT, 1], F32, name="bias_t")
        nc.sync.dma_start(bias_t[:], t_bout)

        identity = held.tile([P, P], BF16, name="identity")
        make_identity(nc, identity[:])

        warm = held.tile([P, 1], F32, name="warm")
        nc.vector.memset(warm[:], 0.0)
        nc.scalar.activation(warm[:], warm[:], EXP)

        window = held.tile([D, S], BF16, name="window")
        for b in range(BLOCKS):
            flipped = psum.tile([D, P], BF16, name=f"flipped{b}", tag=f"bank{b}")
            nc.tensor.transpose(flipped[:], samples[b][:], identity[:])
            nc.vector.tensor_copy(window[:, b * P : (b + 1) * P], flipped[:])

        hs_sums = [psum.tile([HID, HALF], F32, name=f"hs_sum{i}") for i in range(len(HALVES))]
        for i, hs_sum in enumerate(hs_sums):
            piece = offsets[:, i * (HALF // 16) : (i + 1) * (HALF // 16)]
            nc.tensor.matmul(hs_sum[:], w_in[:, 0:HID], window[:].indirect(piece))
        ht_sum = psum.tile([HID, N], F32, name="ht_sum")
        nc.tensor.matmul(ht_sum[:], w_in[:, HID : 2 * HID], window[:].indirect(offsets[:]))


        h_s = held.tile([HID, N], BF16, name="h_s")
        for q, cols in enumerate(QUARTERS):
            in_half = slice((q % 2) * QUARTER, (q % 2 + 1) * QUARTER)
            nc.vector.tensor_scalar(h_s[:, cols], hs_sums[q // 2][:, in_half], bias_h[:, 0:1], 0.0, ADD, MAX)
        h_t = held.tile([HID, N], BF16, name="h_t")
        nc.scalar.activation(h_t[:], ht_sum[:], RELU, bias=bias_h[:, 1:2])

        s_sums = [psum.tile([DOUT, QUARTER], F32, name=f"s_sum{q}", tag=f"bank{q}") for q in range(len(QUARTERS))]
        for s_sum, cols in zip(s_sums, QUARTERS):
            nc.tensor.matmul(s_sum[:], w_s[:], h_s[:, cols])
        t_sum = psum.tile([DOUT, N], F32, name="t_sum")
        nc.tensor.matmul(t_sum[:], w_t[:], h_t[:])

        scale = held.tile([DOUT, N], F32, name="scale")
        for s_sum, cols in zip(s_sums, QUARTERS):
            nc.scalar.activation(scale[:, cols], s_sum[:], EXP, bias=bias_s[:])
        clamped = held.tile([DOUT, N], F32, name="clamped")
        for cols in QUARTERS:
            nc.vector.tensor_scalar(clamped[:, cols], scale[:, cols], math.exp(-CLAMP), math.exp(CLAMP), MAX, MIN)
        scaled = held.tile([DOUT, N], F32, name="scaled")
        for cols in QUARTERS:
            nc.vector.tensor_tensor(scaled[:, cols], clamped[:, cols], other_half[:, cols], MULT)
        results = [held.tile([DOUT, HALF], F32, name=f"result{i}") for i in range(len(HALVES))]
        for q, cols in enumerate(QUARTERS):
            in_half = slice((q % 2) * QUARTER, (q % 2 + 1) * QUARTER)
            nc.vector.scalar_tensor_tensor(
                results[q // 2][:, in_half], t_sum[:, cols], bias_t[:], scaled[:, cols], ADD, ADD
            )
        for result, cols in zip(results, HALVES):
            nc.sync.dma_start(out[:, cols], result[:])
